import numpy as np
import ml_dtypes


def mxq(x, axis, fmt="e4m3"):
    dtype, down = {"e4m3": (ml_dtypes.float8_e4m3fn, 7), "e5m2": (ml_dtypes.float8_e5m2, 14)}[fmt]
    v = np.moveaxis(np.asarray(x, np.float32).astype(ml_dtypes.bfloat16).astype(np.float64), axis, -1)
    blocks = v.reshape(v.shape[:-1] + (-1, 32))
    amax = np.abs(blocks).max(-1, keepdims=True)
    byte = np.maximum(np.where(amax > 0, np.frexp(amax)[1] - 1 + 127, 0) - down, 1)
    scale = np.exp2(byte - 127.0)
    codes = (blocks / scale).astype(np.float32).astype(dtype).astype(np.float64)
    return np.moveaxis((codes * scale).reshape(v.shape), -1, axis)


WIDE = False


def mx_kscale(k):
    if not WIDE:
        return np.ones(k)
    levels = np.array([10, -10, 5, -5, 0])
    if k % 512:
        return np.exp2(np.random.permutation(np.resize(levels, k // 32))).repeat(32)
    a = np.empty((k // 512, 16))
    for p in range(k // 512):
        a[p, :8] = np.random.permutation(np.resize(levels, 8))
        for g in range(8):
            far = levels[np.abs(levels - a[p, g]) >= 10]
            a[p, g + 8] = far[np.random.randint(len(far))]
    return np.exp2(a.ravel()).repeat(32)


BF16 = ml_dtypes.bfloat16


def bf(x):
    return np.asarray(x, np.float32).astype(BF16)


def f64(x):
    return np.asarray(x).astype(np.float64)


B, N, HID, ITERS = 512, 32, 2048, 10
DOUT = N * N
SLOPE = 0.01
EPS = 1e-8


def leaky(v):
    return np.where(v >= 0.0, v, SLOPE * v)


def l1_normalize(r, axis):
    return r / np.maximum(np.abs(r).sum(axis=axis, keepdims=True), EPS)


def draw0():
    s, t = mx_kscale(HID), mx_kscale(HID)
    return {"h3": bf(leaky(np.random.standard_normal((B, HID)) * 1.1) * s),
            "W4": bf(np.random.standard_normal((HID, HID)) * 1.4 / np.sqrt(HID) / s[:, None] * t),
            "b4": bf(np.random.standard_normal(HID) * 0.3 * t),
            "W5": bf(np.random.standard_normal((HID, DOUT)) * 2.0 / np.sqrt(HID) / t[:, None]),
            "b5": bf(np.random.standard_normal(DOUT) * 3.0 - 4.0)}


def core(h3, W4, b4, W5, b5):
    h4 = leaky((mxq(f64(h3), 1, "e4m3") @ mxq(f64(W4), 0, "e4m3")) + f64(b4))
    r = ((mxq(h4, 1, "e4m3") @ mxq(f64(W5), 0, "e4m3")) + f64(b5)).reshape(B, N, N)
    r = np.logaddexp(r, 0.0)
    for _ in range(ITERS):
        r = l1_normalize(r, 1)
        r = l1_normalize(r, 2)
    return r


def e4m3fn_bytes(y):
    return np.clip(np.asarray(y, np.float64), -448.0, 448.0).astype(np.float32).astype(ml_dtypes.float8_e4m3fn).view(np.uint8)


def e4m3fn_values(b):
    return np.asarray(b, np.uint8).view(ml_dtypes.float8_e4m3fn).astype(np.float64)


def setup_inputs():
    d = draw0()
    x0 = np.asarray(d['W5']).astype(np.float64)
    s = (np.max(np.abs(x0), axis=(1,), keepdims=True) / 448.0).astype(np.float32)
    out = {}
    for k, v in d.items():
        if k == 'W5':
            out['W5_bytes'] = e4m3fn_bytes(x0 / s.astype(np.float64))
            out['W5_scale'] = s
        else:
            out[k] = v
    return out


def reference(h3, W4, b4, W5_bytes, W5_scale, b5):
    return core(h3, W4, b4, e4m3fn_values(W5_bytes) * W5_scale.astype(np.float64), b5)

@@ -1,0 +1,324 @@
+from contextlib import ExitStack
+
+import concourse.mybir as mybir
+from concourse.masks import make_identity
+
+B, HID, N = 512, 2048, 32
+DOUT = N * N
+ITERS = 10
+SLOPE = 0.01
+EPS = 1e-8
+
+FLOPS = 2 * B * HID * (HID + DOUT)
+
+P = 128
+PACK = 4
+KP = P * PACK
+G = HID // KP
+TT = B // P
+HALF = 512
+NCH = 8
+BLK = 16
+NMOV = 28
+SEQ = NCH * BLK
+
+F32 = mybir.dt.float32
+BF16 = mybir.dt.bfloat16
+U32 = mybir.dt.uint32
+U8 = mybir.dt.uint8
+X4 = mybir.dt.float8_e4m3fn_x4
+FP8 = mybir.dt.float8_e4m3fn
+ACT = mybir.ActivationFunctionType
+ALU = mybir.AluOpType
+
+
+def tile_matchingnet_pa_kernel(tc, h3, W4, b4, W5_bytes, W5_scale, b5, out):
+    nc = tc.nc
+    with ExitStack() as ctx:
+        keep = ctx.enter_context(tc.tile_pool(name="keep", bufs=1))
+        psum = ctx.enter_context(tc.psum_pool(name="psum", bufs=8))
+
+        ident = keep.tile([P, P], F32, name="ident")
+        make_identity(nc, ident[:])
+        ones = keep.tile([P, 1], F32, name="ones")
+        nc.gpsimd.memset(ones[:], 1.0)
+        b4h = keep.tile([P, G, PACK], BF16, name="b4h")
+        b4c = keep.tile([P, G * PACK], F32, name="b4c")
+        sc5 = keep.tile([P, G, PACK], F32, name="sc5")
+        b5r = keep.tile([P, DOUT], BF16, name="b5r")
+
+        h3c = [keep.tile([P, B], U32, name="h3c%d" % g, align_bytes=64) for g in range(G)]
+        h3s = [keep.tile([P, B], U8, name="h3s%d" % g, align_bytes=64) for g in range(G)]
+        w5c = [keep.tile([P, DOUT], U32, name="w5c%d" % g, align_bytes=64) for g in range(G)]
+        w5s = [keep.tile([P, DOUT], U8, name="w5s%d" % g, align_bytes=64) for g in range(G)]
+        h4c = [keep.tile([P, B], U32, name="h4c%d" % g, align_bytes=64) for g in range(G)]
+        h4s = [keep.tile([P, B], U8, name="h4s%d" % g, align_bytes=64) for g in range(G)]
+
+        with ExitStack() as fctx:
+            front = fctx.enter_context(tc.tile_pool(name="front", bufs=1))
+            hraw = [front.tile([P, HID], BF16, name="hraw%d" % m) for m in range(TT)]
+            gx = front.tile([P, G, B, PACK], BF16, name="gx", align_bytes=64)
+
+            def load_w4(c, g):
+                raw = front.tile([P, PACK, HALF], BF16, name="w4raw", bufs=8)
+                nc.sync.dma_start(
+                    out=raw[:],
+                    in_=W4[KP * g : KP * (g + 1), HALF * c : HALF * (c + 1)].rearrange("(p j) n -> p j n", j=PACK),
+                )
+                return raw
+
+            def load_w5(g):
+                byt = front.tile([P, PACK, DOUT], U8, name="w5b", bufs=2)
+                nc.sync.dma_start(out=byt[:], in_=W5_bytes[KP * g : KP * (g + 1), :].rearrange("(p j) n -> p j n", j=PACK))
+                return byt
+
+            nc.scalar.dma_start(out=b4h[:], in_=b4.rearrange("(g p j) -> p g j", p=P, j=PACK))
+            nc.scalar.dma_start(out=sc5[:], in_=W5_scale.rearrange("(g p j) o -> p g (j o)", p=P, j=PACK))
+            nc.gpsimd.tensor_copy(out=b4c[:], in_=b4h[:].rearrange("p g j -> p (g j)"))
+
+            w4raw = {}
+            w5byt = {}
+            w4raw[0, 0] = load_w4(0, 0)
+            nc.sync.dma_start(out=hraw[0][:], in_=h3[0:P, :])
+            w4raw[0, 1] = load_w4(0, 1)
+            for m in range(1, TT):
+                nc.sync.dma_start(out=hraw[m][:], in_=h3[P * m : P * (m + 1), :])
+            w5byt[0] = load_w5(0)
+            w4raw[0, 2] = load_w4(0, 2)
+            w4raw[0, 3] = load_w4(0, 3)
+
+            def h3_tile(m):
+                words = hraw[m][:].bitcast(F32)
+                gxw = gx[:].bitcast(F32)
+                for gp in range(G // 2):
+                    bank = psum.tile([P, HALF], F32, name="bank")
+                    for gg in range(2):
+                        for u in range(2):
+                            g = 2 * gp + gg
+                            s = 2 * gg + u
+                            nc.tensor.transpose(
+                                bank[:, P * s : P * (s + 1)], words[:, 256 * g + u : 256 * (g + 1) : 2], ident[:]
+                            )
+                    for gg in range(2):
+                        nc.scalar.copy(
+                            out=gxw[:, 2 * gp + gg, P * m : P * (m + 1), :],
+                            in_=bank[:, 256 * gg : 256 * (gg + 1)].rearrange("p (u r) -> p r u", u=2),
+                        )
+
+            def prep_w4(c, g, codes, scales):
+                raw = w4raw.pop((c, g))
+                grp = front.tile([P, PACK, P, PACK], BF16, name="w4grp", bufs=4, align_bytes=64)
+                src = raw[:].rearrange("p j (m t) -> p t m j", t=PACK)
+                nc.vector.tensor_copy(out=grp[:, 0:2], in_=src[:, 0:2])
+                nc.scalar.copy(out=grp[:, 2:4], in_=src[:, 2:4])
+                nc.vector.quantize_mx(
+                    out=codes[:].bitcast(X4), scales=scales[:], in_=grp[:].rearrange("p t m j -> p (t m j)")
+                )
+
+            def prep_w5(g):
+                byt = w5byt.pop(g)
+                wide = front.tile([P, PACK, DOUT], BF16, name="w5p", bufs=2)
+                for j in range(PACK):
+                    nc.scalar.activation(
+                        out=wide[:, j, :], in_=byt[:, j, :].bitcast(FP8), func=ACT.Copy, scale=sc5[:, g, j : j + 1]
+                    )
+                for h in range(2):
+                    grp = front.tile([P, HALF, PACK], BF16, name="w5g", bufs=3, align_bytes=64)
+                    nc.vector.tensor_copy(
+                        out=grp[:], in_=wide[:, :, HALF * h : HALF * (h + 1)].rearrange("p j n -> p n j")
+                    )
+                    cols = slice(HALF * h, HALF * (h + 1))
+                    nc.vector.quantize_mx(
+                        out=w5c[g][:, cols].bitcast(X4), scales=w5s[g][:, cols], in_=grp[:].rearrange("p n j -> p (n j)")
+                    )
+
+            for m in range(TT):
+                h3_tile(m)
+            for g in range(G):
+                nc.vector.quantize_mx(
+                    out=h3c[g][:].bitcast(X4), scales=h3s[g][:], in_=gx[:, g].rearrange("p n t -> p (n t)")
+                )
+
+            def front_chunk(c):
+                codes = []
+                scales = []
+                for g in range(G):
+                    cw = front.tile([P, HALF], U32, name="w4c%d" % g, bufs=2, align_bytes=64)
+                    sw = front.tile([P, HALF], U8, name="w4s%d" % g, bufs=2, align_bytes=64)
+                    prep_w4(c, g, cw, sw)
+                    codes.append(cw)
+                    scales.append(sw)
+                y = front.tile([P, PACK, B], F32, name="y", bufs=2)
+                for t in range(PACK):
+                    bank = psum.tile([P, HALF], F32, name="bank")
+                    mc = slice(P * t, P * (t + 1))
+                    for g in range(G):
+                        nc.tensor.matmul_mx(
+                            out=bank[:],
+                            lhsT=codes[g][:, mc].bitcast(X4),
+                            lhsT_scale=scales[g][:, mc],
+                            rhs=h3c[g][:].bitcast(X4),
+                            rhs_scale=h3s[g][:],
+                            start=(g == 0),
+                            stop=(g == G - 1),
+                        )
+                    nc.scalar.activation(
+                        out=y[:, t, :], in_=bank[:], func=ACT.Identity, bias=b4c[:, PACK * c + t : PACK * c + t + 1]
+                    )
+                hb = front.tile([P, B, PACK], BF16, name="hb", bufs=2, align_bytes=64)
+                yv = y[:].rearrange("p t n -> p n t")
+                nc.vector.scalar_tensor_tensor(out=hb[:], in0=yv, scalar=SLOPE, in1=yv, op0=ALU.mult, op1=ALU.max)
+                nc.vector.quantize_mx(
+                    out=h4c[c][:].bitcast(X4), scales=h4s[c][:], in_=hb[:].rearrange("p n t -> p (n t)")
+                )
+
+            for c in range(G):
+                if c + 1 < G:
+                    for g in range(G):
+                        w4raw[c + 1, g] = load_w4(c + 1, g)
+                    w5byt[c + 1] = load_w5(c + 1)
+                if c == G - 1:
+                    nc.sync.dma_start(out=b5r[:], in_=b5.partition_broadcast(P))
+                prep_w5(c)
+                front_chunk(c)
+
+        late = ctx.enter_context(tc.tile_pool(name="late", bufs=1))
+
+        def logits(m):
+            z = late.tile([P, DOUT], F32, name="z", bufs=4)
+            for h in range(2):
+                bank = psum.tile([P, HALF], F32, name="bank")
+                cols = slice(HALF * h, HALF * (h + 1))
+                for g in range(G):
+                    nc.tensor.matmul_mx(
+                        out=bank[:],
+                        lhsT=h4c[g][:, P * m : P * (m + 1)].bitcast(X4),
+                        lhsT_scale=h4s[g][:, P * m : P * (m + 1)],
+                        rhs=w5c[g][:, cols].bitcast(X4),
+                        rhs_scale=w5s[g][:, cols],
+                        start=(g == 0),
+                        stop=(g == G - 1),
+                    )
+                nc.vector.tensor_tensor(out=z[:, cols], in0=bank[:], in1=b5r[:, cols], op=ALU.add)
+            return z
+
+        def exps(z):
+            e = late.tile([P, DOUT], F32, name="e", bufs=2)
+            nc.scalar.activation(out=e[:], in_=z[:], func=ACT.Exp)
+            return e
+
+        def logs(e):
+            nc.scalar.activation(out=e[:], in_=e[:], func=ACT.Ln, bias=ones[:, 0:1])
+            return e
+
+        def blocks(z, l, m):
+            K = late.tile([P, DOUT], F32, name="K", bufs=2, align_bytes=64)
+            nc.vector.scalar_tensor_tensor(out=K[:], in0=l[:], scalar=40.0, in1=z[:], op0=ALU.min, op1=ALU.max)
+            Yp = late.tile([P, DOUT], F32, name="Yp", bufs=4, align_bytes=64)
+            nc.vector.transpose(out=Yp[:], in_=K[:])
+            Yc = late.tile([P, DOUT], F32, name="Yc", bufs=4, align_bytes=64)
+            nc.vector.tensor_scalar(
+                out=Yc[:].rearrange("p (b i) -> p b i", i=N),
+                in0=Yp[:].rearrange("p (i b) -> p b i", b=N),
+                scalar1=1e-20,
+                scalar2=None,
+                op0=ALU.max,
+            )
+            Xc = late.tile([P, DOUT], F32, name="Xc", bufs=4, align_bytes=64)
+            for h in range(2):
+                bank = psum.tile([P, HALF], F32, name="bank")
+                for c in range(4):
+                    c8 = 4 * h + c
+                    nc.tensor.transpose(bank[:, P * c : P * (c + 1)], Yc[:, P * c8 : P * (c8 + 1)], ident[:])
+                nc.scalar.copy(out=Xc[:, HALF * h : HALF * (h + 1)], in_=bank[:])
+            ub = late.tile([P, SEQ + BLK], F32, name="ub", bufs=4)
+            vb = late.tile([P, SEQ + BLK], F32, name="vb", bufs=4)
+            nc.gpsimd.memset(ub[:], 0.0)
+            nc.gpsimd.memset(vb[:], 0.0)
+            for q in range(4):
+                nc.gpsimd.memset(
+                    ub[32 * q : 32 * q + 32, 0:SEQ].rearrange("p (c a b) -> p c a b", a=4, b=4)[:, :, q, :], 1.0
+                )
+            wu = late.tile([P, N], F32, name="wu", bufs=4)
+            wv = late.tile([P, N], F32, name="wv", bufs=4)
+            nc.gpsimd.memset(wu[:], 1.0)
+            nc.gpsimd.memset(wv[:], 1.0)
+            return dict(Yp=Yp, Yc=Yc, Xc=Xc, ub=ub, vb=vb, wu=wu, wv=wv, m=m)
+
+        def half_step(mat, src, dst, w):
+            bank = psum.tile([P, HALF], F32, name="bank")
+            for c in range(NCH):
+                nc.tensor.matmul(
+                    out=bank[:, BLK * c : BLK * c + NMOV],
+                    lhsT=mat[:, P * c : P * (c + 1)],
+                    rhs=src[:, BLK * c : BLK * c + NMOV],
+                    start=True,
+                    stop=True,
+                )
+            for q in range(4):
+                rows = slice(32 * q, 32 * q + 32)
+                nc.vector.scalar_tensor_tensor(
+                    out=w[rows, :], in0=w[rows, :], scalar=EPS, in1=bank[rows, q:SEQ:4], op0=ALU.mult, op1=ALU.max
+                )
+            v = late.tile([P, N], F32, name="v", bufs=8)
+            nc.vector.reciprocal(out=v[:], in_=w[:])
+            if dst is not None:
+                for q in range(4):
+                    rows = slice(32 * q, 32 * q + 32)
+                    nc.scalar.copy(
+                        out=dst[rows, 0:SEQ].rearrange("p (c a b) -> p c a b", a=4, b=4)[:, :, q, :],
+                        in_=v[rows, :].rearrange("p (c b) -> p c b", b=4),
+                    )
+            return v
+
+        def v_step(s):
+            s["v"] = half_step(s["Xc"], s["ub"], s["vb"], s["wv"])
+
+        def u_step(s, last):
+            s["u"] = half_step(s["Yc"], s["vb"], None if last else s["ub"], s["wu"])
+
+        def scale_v(s):
+            a = late.tile([P, N, N], F32, name="a", bufs=2)
+            nc.vector.tensor_tensor(
+                out=a[:],
+                in0=s["Yp"][:].rearrange("p (i b) -> p i b", b=N),
+                in1=s["v"][:].unsqueeze(1).to_broadcast([P, N, N]),
+                op=ALU.mult,
+            )
+            s["a"] = a
+
+        def finish(s):
+            ubc = late.tile([P, N, N], F32, name="ubc", bufs=2)
+            nc.scalar.copy(out=ubc[:], in_=s["u"][:].unsqueeze(2).to_broadcast([P, N, N]))
+            uw = ubc[:].rearrange("p c j -> p (c j)")
+            rr = late.tile([P, N, N], F32, name="rr", bufs=2, align_bytes=64)
+            for h in range(2):
+                bank = psum.tile([P, HALF], F32, name="bank")
+                for c in range(4):
+                    c8 = 4 * h + c
+                    nc.tensor.transpose(bank[:, P * c : P * (c + 1)], uw[:, P * c8 : P * (c8 + 1)], ident[:])
+                bs = slice(16 * h, 16 * h + 16)
+                nc.vector.tensor_tensor(
+                    out=rr[:, :, bs], in0=bank[:].rearrange("p (b i) -> p i b", i=N), in1=s["a"][:, :, bs], op=ALU.mult
+                )
+            fin = late.tile([P, DOUT], F32, name="fin", bufs=2, align_bytes=64)
+            nc.vector.transpose(out=fin[:], in_=rr[:].rearrange("p i b -> p (i b)"))
+            m = s["m"]
+            nc.sync.dma_start(out=out[P * m : P * (m + 1)].rearrange("b i j -> b (i j)"), in_=fin[:])
+
+        zs = [logits(m) for m in range(TT)]
+        for pair in range(2):
+            ms = [2 * pair, 2 * pair + 1]
+            es = [exps(zs[m]) for m in ms]
+            ls = [logs(e) for e in es]
+            st = [blocks(zs[m], l, m) for m, l in zip(ms, ls)]
+            for it in range(ITERS):
+                for s in st:
+                    v_step(s)
+                if it == ITERS - 1:
+                    for s in st:
+                        scale_v(s)
+                for s in st:
+                    u_step(s, it == ITERS - 1)
+            for s in st:
+                finish(s)

@@ -18,9 +18,7 @@ G = HID // KP
 TT = B // P
 HALF = 512
 NCH = 8
-BLK = 16
-NMOV = 28
-SEQ = NCH * BLK
+NBANK = 7
 
 F32 = mybir.dt.float32
 BF16 = mybir.dt.bfloat16
@@ -36,10 +34,31 @@ def tile_matchingnet_pa_kernel(tc, h3, W4, b4, W5_bytes, W5_scale, b5, out):
     nc = tc.nc
     with ExitStack() as ctx:
         keep = ctx.enter_context(tc.tile_pool(name="keep", bufs=1))
-        psum = ctx.enter_context(tc.psum_pool(name="psum", bufs=8))
+        psum = ctx.enter_context(tc.psum_pool(name="psum", bufs=1))
 
         ident = keep.tile([P, P], F32, name="ident")
         make_identity(nc, ident[:])
+        identb = keep.tile([P, P], BF16, name="identb")
+        make_identity(nc, identb[:])
+        par = keep.tile([P, 2], F32, name="par")
+        idq = ident[:].rearrange("p (a b r) -> p b a r", a=2, b=2)
+        nc.vector.tensor_reduce(out=par[:], in_=idq, axis=mybir.AxisListType.XY, op=ALU.add)
+        pv = keep.tile([P, P], F32, name="pv")
+        pu = keep.tile([P, P], F32, name="pu")
+        pf = keep.tile([P, P], F32, name="pf")
+        nc.gpsimd.tensor_copy(
+            out=pf[:].rearrange("p (b c k) -> p b c k", b=4, c=NCH), in_=ident[:].rearrange("p (k c b) -> p b c k", k=4, c=NCH)
+        )
+        pvv = pv[:].rearrange("p (h e c a k) -> p h e c a k", h=2, e=2, c=NCH, a=2)
+        puv = pu[:].rearrange("p (h e c a k) -> p h e c a k", h=2, e=2, c=NCH, a=2)
+        iv = ident[:].rearrange("p (h e c g a) -> p h e c g a", h=2, e=2, c=NCH, g=2)
+        iu = ident[:].rearrange("p (a k c g x) -> p x k c a g", a=2, k=2, c=NCH, g=2)
+        for e in range(2):
+            for k in range(2):
+                g = (e + k) % 2
+                for x in range(2):
+                    nc.gpsimd.tensor_copy(out=pvv[:, x, e, :, :, k], in_=iv[:, x, e, :, g, :])
+                    nc.gpsimd.tensor_copy(out=puv[:, x, e, :, :, k], in_=iu[:, x, k, :, :, g])
         ones = keep.tile([P, 1], F32, name="ones")
         nc.gpsimd.memset(ones[:], 1.0)
         b4h = keep.tile([P, G, PACK], BF16, name="b4h")
@@ -78,20 +97,18 @@ def tile_matchingnet_pa_kernel(tc, h3, W4, b4, W5_bytes, W5_scale, b5, out):
 
             w4raw = {}
             w5byt = {}
-            w4raw[0, 0] = load_w4(0, 0)
-            nc.sync.dma_start(out=hraw[0][:], in_=h3[0:P, :])
-            w4raw[0, 1] = load_w4(0, 1)
-            for m in range(1, TT):
-                nc.sync.dma_start(out=hraw[m][:], in_=h3[P * m : P * (m + 1), :])
             w5byt[0] = load_w5(0)
-            w4raw[0, 2] = load_w4(0, 2)
-            w4raw[0, 3] = load_w4(0, 3)
+            w4raw[0, 0] = load_w4(0, 0)
+            for m in range(TT):
+                nc.sync.dma_start(out=hraw[m][:], in_=h3[P * m : P * (m + 1), :])
+            for g in range(1, G):
+                w4raw[0, g] = load_w4(0, g)
 
             def h3_tile(m):
                 words = hraw[m][:].bitcast(F32)
                 gxw = gx[:].bitcast(F32)
                 for gp in range(G // 2):
-                    bank = psum.tile([P, HALF], F32, name="bank")
+                    bank = psum.tile([P, HALF], F32, name="bank", bufs=NBANK)
                     for gg in range(2):
                         for u in range(2):
                             g = 2 * gp + gg
@@ -132,6 +149,7 @@ def tile_matchingnet_pa_kernel(tc, h3, W4, b4, W5_bytes, W5_scale, b5, out):
                         out=w5c[g][:, cols].bitcast(X4), scales=w5s[g][:, cols], in_=grp[:].rearrange("p n j -> p (n j)")
                     )
 
+            prep_w5(0)
             for m in range(TT):
                 h3_tile(m)
             for g in range(G):
@@ -149,12 +167,12 @@ def tile_matchingnet_pa_kernel(tc, h3, W4, b4, W5_bytes, W5_scale, b5, out):
                     codes.append(cw)
                     scales.append(sw)
                 y = front.tile([P, PACK, B], F32, name="y", bufs=2)
-                for t in range(PACK):
-                    bank = psum.tile([P, HALF], F32, name="bank")
-                    mc = slice(P * t, P * (t + 1))
-                    for g in range(G):
+                banks = [psum.tile([P, HALF], F32, name="bank", bufs=NBANK) for t in range(PACK)]
+                for g in range(G):
+                    for t in range(PACK):
+                        mc = slice(P * t, P * (t + 1))
                         nc.tensor.matmul_mx(
-                            out=bank[:],
+                            out=banks[t][:],
                             lhsT=codes[g][:, mc].bitcast(X4),
                             lhsT_scale=scales[g][:, mc],
                             rhs=h3c[g][:].bitcast(X4),
@@ -162,15 +180,25 @@ def tile_matchingnet_pa_kernel(tc, h3, W4, b4, W5_bytes, W5_scale, b5, out):
                             start=(g == 0),
                             stop=(g == G - 1),
                         )
+                for t in range(PACK):
                     nc.scalar.activation(
-                        out=y[:, t, :], in_=bank[:], func=ACT.Identity, bias=b4c[:, PACK * c + t : PACK * c + t + 1]
+                        out=y[:, t, :],
+                        in_=banks[t][:],
+                        func=ACT.Identity,
+                        bias=b4c[:, PACK * c + t : PACK * c + t + 1],
                     )
                 hb = front.tile([P, B, PACK], BF16, name="hb", bufs=2, align_bytes=64)
                 yv = y[:].rearrange("p t n -> p n t")
-                nc.vector.scalar_tensor_tensor(out=hb[:], in0=yv, scalar=SLOPE, in1=yv, op0=ALU.mult, op1=ALU.max)
-                nc.vector.quantize_mx(
-                    out=h4c[c][:].bitcast(X4), scales=h4s[c][:], in_=hb[:].rearrange("p n t -> p (n t)")
-                )
+                for h in range(2):
+                    tok = slice(256 * h, 256 * (h + 1))
+                    nc.vector.scalar_tensor_tensor(
+                        out=hb[:, tok], in0=yv[:, tok], scalar=SLOPE, in1=yv[:, tok], op0=ALU.mult, op1=ALU.max
+                    )
+                    nc.vector.quantize_mx(
+                        out=h4c[c][:, tok].bitcast(X4),
+                        scales=h4s[c][:, tok],
+                        in_=hb[:, tok].rearrange("p n t -> p (n t)"),
+                    )
 
             for c in range(G):
                 if c + 1 < G:
@@ -179,19 +207,20 @@ def tile_matchingnet_pa_kernel(tc, h3, W4, b4, W5_bytes, W5_scale, b5, out):
                     w5byt[c + 1] = load_w5(c + 1)
                 if c == G - 1:
                     nc.sync.dma_start(out=b5r[:], in_=b5.partition_broadcast(P))
-                prep_w5(c)
                 front_chunk(c)
+                if c > 0:
+                    prep_w5(c)
 
         late = ctx.enter_context(tc.tile_pool(name="late", bufs=1))
 
         def logits(m):
             z = late.tile([P, DOUT], F32, name="z", bufs=4)
-            for h in range(2):
-                bank = psum.tile([P, HALF], F32, name="bank")
-                cols = slice(HALF * h, HALF * (h + 1))
-                for g in range(G):
+            banks = [psum.tile([P, HALF], F32, name="bank", bufs=NBANK) for h in range(2)]
+            for g in range(G):
+                for h in range(2):
+                    cols = slice(HALF * h, HALF * (h + 1))
                     nc.tensor.matmul_mx(
-                        out=bank[:],
+                        out=banks[h][:],
                         lhsT=h4c[g][:, P * m : P * (m + 1)].bitcast(X4),
                         lhsT_scale=h4s[g][:, P * m : P * (m + 1)],
                         rhs=w5c[g][:, cols].bitcast(X4),
@@ -199,24 +228,37 @@ def tile_matchingnet_pa_kernel(tc, h3, W4, b4, W5_bytes, W5_scale, b5, out):
                         start=(g == 0),
                         stop=(g == G - 1),
                     )
-                nc.vector.tensor_tensor(out=z[:, cols], in0=bank[:], in1=b5r[:, cols], op=ALU.add)
+            for h in range(2):
+                cols = slice(HALF * h, HALF * (h + 1))
+                nc.vector.tensor_tensor(out=z[:, cols], in0=banks[h][:], in1=b5r[:, cols], op=ALU.add)
             return z
 
         def exps(z):
-            e = late.tile([P, DOUT], F32, name="e", bufs=2)
+            e = late.tile([P, DOUT], F32, name="e", bufs=4)
             nc.scalar.activation(out=e[:], in_=z[:], func=ACT.Exp)
             return e
 
         def logs(e):
             nc.scalar.activation(out=e[:], in_=e[:], func=ACT.Ln, bias=ones[:, 0:1])
-            return e
+
+        def mov(t, rows, R):
+            return t[rows, :].rearrange("p (s t h x) -> p s t h x", t=2, h=R, x=R)
+
+        def transposes(dst, src, n):
+            for h in range(n // 8):
+                bank = psum.tile([P, HALF], F32, name="bank", bufs=NBANK)
+                bb = bank[:].bitcast(BF16)
+                for c in range(8):
+                    nc.tensor.transpose(bb[:, P * c : P * (c + 1)], src[:, 8 * h + c, :], identb[:])
+                nc.scalar.copy(out=dst[:, DOUT * h : DOUT * (h + 1)], in_=bb)
 
         def blocks(z, l, m):
-            K = late.tile([P, DOUT], F32, name="K", bufs=2, align_bytes=64)
+            R = 4 if m == 0 else 2
+            K = late.tile([P, DOUT], F32, name="K", bufs=4, align_bytes=64)
             nc.vector.scalar_tensor_tensor(out=K[:], in0=l[:], scalar=40.0, in1=z[:], op0=ALU.min, op1=ALU.max)
-            Yp = late.tile([P, DOUT], F32, name="Yp", bufs=4, align_bytes=64)
+            Yp = late.tile([P, DOUT], F32, name="Yp", bufs=2, align_bytes=64)
             nc.vector.transpose(out=Yp[:], in_=K[:])
-            Yc = late.tile([P, DOUT], F32, name="Yc", bufs=4, align_bytes=64)
+            Yc = late.tile([P, DOUT], F32, name="Yc", bufs=2)
             nc.vector.tensor_scalar(
                 out=Yc[:].rearrange("p (b i) -> p b i", i=N),
                 in0=Yp[:].rearrange("p (i b) -> p b i", b=N),
@@ -224,101 +266,159 @@ def tile_matchingnet_pa_kernel(tc, h3, W4, b4, W5_bytes, W5_scale, b5, out):
                 scalar2=None,
                 op0=ALU.max,
             )
-            Xc = late.tile([P, DOUT], F32, name="Xc", bufs=4, align_bytes=64)
-            for h in range(2):
-                bank = psum.tile([P, HALF], F32, name="bank")
-                for c in range(4):
-                    c8 = 4 * h + c
-                    nc.tensor.transpose(bank[:, P * c : P * (c + 1)], Yc[:, P * c8 : P * (c8 + 1)], ident[:])
-                nc.scalar.copy(out=Xc[:, HALF * h : HALF * (h + 1)], in_=bank[:])
-            ub = late.tile([P, SEQ + BLK], F32, name="ub", bufs=4)
-            vb = late.tile([P, SEQ + BLK], F32, name="vb", bufs=4)
+            hl = late.tile([P, 2, DOUT], BF16, name="hl", bufs=3)
+            nc.scalar.copy(out=hl[:, 0], in_=Yc[:])
+            nc.vector.tensor_tensor(out=hl[:, 1], in0=Yc[:], in1=hl[:, 0], op=ALU.subtract)
+            if R == 4:
+                ys = hl[:].rearrange("p w (c n) -> p (w c) n", n=P)
+                xt = late.tile([P, 2 * NCH * P], BF16, name="xt")
+            else:
+                yt = late.tile([P, 2 * NCH, 2, P], BF16, name="yt", bufs=3)
+                src = hl[:].rearrange("p w (c a k i) -> p (w c) a k i", a=2, k=2, i=N)
+                for sg in range(2):
+                    for kp in range(2):
+                        r = (sg + kp) % 2
+                        nc.vector.tensor_scalar(
+                            out=yt[:, :, sg, :].rearrange("p w (a k i) -> p w a k i", a=2, k=2)[:, :, :, kp, :],
+                            in0=src[:, :, :, kp, :],
+                            scalar1=par[:, r : r + 1],
+                            scalar2=None,
+                            op0=ALU.mult,
+                        )
+                ys = yt[:].rearrange("p w g n -> p (w g) n")
+                xt = late.tile([P, 4 * NCH * P], BF16, name="xh", bufs=3)
+            return dict(K=K, ys=ys, xt=xt, m=m, R=R)
+
+        def state(s):
+            R, m, xt = s["R"], s["m"], s["xt"]
+            transposes(xt, s["ys"], 64 // R)
+            ub = late.tile([P, 2 * N * R], BF16, name="ub%d" % m)
+            vb = late.tile([P, 2 * N * R], BF16, name="vb%d" % m)
             nc.gpsimd.memset(ub[:], 0.0)
             nc.gpsimd.memset(vb[:], 0.0)
-            for q in range(4):
-                nc.gpsimd.memset(
-                    ub[32 * q : 32 * q + 32, 0:SEQ].rearrange("p (c a b) -> p c a b", a=4, b=4)[:, :, q, :], 1.0
-                )
-            wu = late.tile([P, N], F32, name="wu", bufs=4)
-            wv = late.tile([P, N], F32, name="wv", bufs=4)
+            for g in range(R):
+                rows = slice(P // R * g, P // R * (g + 1))
+                nc.gpsimd.memset(mov(ub, rows, R)[:, :, 0, g, :], 1.0)
+            wu = late.tile([P, N], F32, name="wu%d" % m, align_bytes=64)
+            wv = late.tile([P, N], F32, name="wv%d" % m, align_bytes=64)
             nc.gpsimd.memset(wu[:], 1.0)
             nc.gpsimd.memset(wv[:], 1.0)
-            return dict(Yp=Yp, Yc=Yc, Xc=Xc, ub=ub, vb=vb, wu=wu, wv=wv, m=m)
+            s["xs"] = xt[:].rearrange("p (w n) -> p w n", n=P)
+            s["ub"], s["vb"], s["wu"], s["wv"] = ub, vb, wu, wv
 
-        def half_step(mat, src, dst, w):
-            bank = psum.tile([P, HALF], F32, name="bank")
-            for c in range(NCH):
-                nc.tensor.matmul(
-                    out=bank[:, BLK * c : BLK * c + NMOV],
-                    lhsT=mat[:, P * c : P * (c + 1)],
-                    rhs=src[:, BLK * c : BLK * c + NMOV],
+        def keep_warm(n):
+            for k in range(n):
+                nc.tensor.matmul_mx(
+                    out=warm[:],
+                    lhsT=h4c[0][:, 0:P].bitcast(X4),
+                    lhsT_scale=h4s[0][:, 0:P],
+                    rhs=w5c[0][:, 0:HALF].bitcast(X4),
+                    rhs_scale=w5s[0][:, 0:HALF],
                     start=True,
                     stop=True,
                 )
-            for q in range(4):
-                rows = slice(32 * q, 32 * q + 32)
-                nc.vector.scalar_tensor_tensor(
-                    out=w[rows, :], in0=w[rows, :], scalar=EPS, in1=bank[rows, q:SEQ:4], op0=ALU.mult, op1=ALU.max
+
+        def half_step(mat, src, dst, w, R):
+            n = R * R
+            ns = N // R
+            bank = psum.tile([P, HALF], F32, name="bank", bufs=NBANK)
+            for s in range(ns):
+                o = 2 * n * s
+                nc.tensor.matmul(
+                    out=bank[:, o : o + 2 * n], lhsT=mat[:, s, :], rhs=src[:, o : o + 2 * n], start=True, stop=False
                 )
-            v = late.tile([P, N], F32, name="v", bufs=8)
+                nc.tensor.matmul(
+                    out=bank[:, o : o + n], lhsT=mat[:, ns + s, :], rhs=src[:, o : o + n], start=False, stop=True
+                )
+            t = late.tile([P, N], F32, name="t", bufs=8)
+            groups = [slice(P // R * g, P // R * (g + 1)) for g in range(R)]
+            for g, rows in enumerate(groups):
+                nc.vector.tensor_reduce(
+                    out=t[rows, :].rearrange("p (s a) -> p s a", a=R),
+                    in_=bank[rows, 0 : 2 * n * ns].rearrange("p (s t a x) -> p s a x t", t=2, a=R, x=R)[:, :, :, g, :],
+                    axis=mybir.AxisListType.X,
+                    op=ALU.add,
+                )
+            nc.vector.scalar_tensor_tensor(out=w[:], in0=w[:], scalar=EPS, in1=t[:], op0=ALU.mult, op1=ALU.max)
+            v = late.tile([P, N], F32, name="v", bufs=8, align_bytes=64)
             nc.vector.reciprocal(out=v[:], in_=w[:])
             if dst is not None:
-                for q in range(4):
-                    rows = slice(32 * q, 32 * q + 32)
+                for g, rows in enumerate(groups):
                     nc.scalar.copy(
-                        out=dst[rows, 0:SEQ].rearrange("p (c a b) -> p c a b", a=4, b=4)[:, :, q, :],
-                        in_=v[rows, :].rearrange("p (c b) -> p c b", b=4),
+                        out=mov(dst, rows, R)[:, :, 0, g, :], in_=v[rows, :].rearrange("p (s a) -> p s a", a=R)
+                    )
+                for g, rows in enumerate(groups):
+                    nc.vector.tensor_tensor(
+                        out=mov(dst, rows, R)[:, :, 1, g, :],
+                        in0=v[rows, :].rearrange("p (s a) -> p s a", a=R),
+                        in1=mov(dst, rows, R)[:, :, 0, g, :],
+                        op=ALU.subtract,
                     )
             return v
 
-        def v_step(s):
-            s["v"] = half_step(s["Xc"], s["ub"], s["vb"], s["wv"])
+        def natural(v, perm):
+            vt = late.tile([P, N], F32, name="vt", bufs=4, align_bytes=64)
+            nc.vector.transpose(out=vt[:], in_=v)
+            bank = psum.tile([P, HALF], F32, name="bank", bufs=NBANK)
+            nc.tensor.matmul(out=bank[:, 0:N], lhsT=perm[:], rhs=vt[:], start=True, stop=True)
+            return bank
 
-        def u_step(s, last):
-            s["u"] = half_step(s["Yc"], s["vb"], None if last else s["ub"], s["wu"])
-
-        def scale_v(s):
-            a = late.tile([P, N, N], F32, name="a", bufs=2)
+        def finish(s, v):
+            vn = natural(v[:], ident if s["R"] == 4 else pv)
+            wn = natural(s["wu"][:], pf if s["R"] == 4 else pu)
+            kv = late.tile([P, N, N], F32, name="kv", bufs=2)
             nc.vector.tensor_tensor(
-                out=a[:],
-                in0=s["Yp"][:].rearrange("p (i b) -> p i b", b=N),
-                in1=s["v"][:].unsqueeze(1).to_broadcast([P, N, N]),
+                out=kv[:],
+                in0=s["K"][:].rearrange("p (i j) -> p i j", j=N),
+                in1=vn[:, 0:N].unsqueeze(1).to_broadcast([P, N, N]),
                 op=ALU.mult,
             )
-            s["a"] = a
-
-        def finish(s):
-            ubc = late.tile([P, N, N], F32, name="ubc", bufs=2)
-            nc.scalar.copy(out=ubc[:], in_=s["u"][:].unsqueeze(2).to_broadcast([P, N, N]))
-            uw = ubc[:].rearrange("p c j -> p (c j)")
-            rr = late.tile([P, N, N], F32, name="rr", bufs=2, align_bytes=64)
-            for h in range(2):
-                bank = psum.tile([P, HALF], F32, name="bank")
-                for c in range(4):
-                    c8 = 4 * h + c
-                    nc.tensor.transpose(bank[:, P * c : P * (c + 1)], uw[:, P * c8 : P * (c8 + 1)], ident[:])
-                bs = slice(16 * h, 16 * h + 16)
-                nc.vector.tensor_tensor(
-                    out=rr[:, :, bs], in0=bank[:].rearrange("p (b i) -> p i b", i=N), in1=s["a"][:, :, bs], op=ALU.mult
-                )
-            fin = late.tile([P, DOUT], F32, name="fin", bufs=2, align_bytes=64)
-            nc.vector.transpose(out=fin[:], in_=rr[:].rearrange("p i b -> p (i b)"))
+            rs = late.tile([P, N], F32, name="rs", bufs=2)
+            nc.vector.tensor_reduce(out=rs[:], in_=kv[:], axis=mybir.AxisListType.X, op=ALU.add)
+            nc.vector.scalar_tensor_tensor(
+                out=rs[:], in0=wn[:, 0:N], scalar=EPS, in1=rs[:], op0=ALU.mult, op1=ALU.max
+            )
+            un = late.tile([P, N], F32, name="un", bufs=2)
+            nc.vector.reciprocal(out=un[:], in_=rs[:])
+            res = late.tile([P, N, N], F32, name="res", bufs=2)
             m = s["m"]
-            nc.sync.dma_start(out=out[P * m : P * (m + 1)].rearrange("b i j -> b (i j)"), in_=fin[:])
+            for h in range(2):
+                ii = slice(16 * h, 16 * h + 16)
+                nc.vector.tensor_tensor(
+                    out=res[:, ii], in0=kv[:, ii], in1=un[:, ii].unsqueeze(2).to_broadcast([P, 16, N]), op=ALU.mult
+                )
+                nc.sync.dma_start(out=out[P * m : P * (m + 1), ii, :], in_=res[:, ii])
 
+        warm = psum.tile([P, HALF], F32, name="warm")
+        SKEW = 0
+        STEPS = 2 * ITERS - 1
         zs = [logits(m) for m in range(TT)]
+        es = [None] * TT
         for pair in range(2):
-            ms = [2 * pair, 2 * pair + 1]
-            es = [exps(zs[m]) for m in ms]
-            ls = [logs(e) for e in es]
-            st = [blocks(zs[m], l, m) for m, l in zip(ms, ls)]
-            for it in range(ITERS):
-                for s in st:
-                    v_step(s)
-                if it == ITERS - 1:
-                    for s in st:
-                        scale_v(s)
-                for s in st:
-                    u_step(s, it == ITERS - 1)
-            for s in st:
-                finish(s)
+            for m in (2 * pair, 2 * pair + 1):
+                es[m] = exps(zs[m])
+            for m in (2 * pair, 2 * pair + 1):
+                logs(es[m])
+        st = [None] * TT
+
+        def one_step(s, h):
+            end = h == STEPS - 1
+            if h % 2 == 0:
+                v = half_step(s["xs"], s["ub"], None if end else s["vb"], s["wv"], s["R"])
+                if end:
+                    finish(s, v)
+            else:
+                half_step(s["ys"], s["vb"], s["ub"], s["wu"], s["R"])
+
+        with tc.manual_schedule(engines={mybir.EngineType.PE}):
+            for r in range(STEPS + SKEW * (TT - 1)):
+                for m in range(TT):
+                    h = r - SKEW * m
+                    if h == 0:
+                        st[m] = blocks(zs[m], es[m], m)
+                        state(st[m])
+                        keep_warm(6)
+                    if 0 <= h < STEPS:
+                        one_step(st[m], h)
+                        if m in (1, 3):
+                            keep_warm(1)

@@ -18,7 +18,9 @@ G = HID // KP
 TT = B // P
 HALF = 512
 NCH = 8
+SEQ = 16 * NCH
 NBANK = 7
+HALVES = (slice(0, 64), slice(64, 128))
 
 F32 = mybir.dt.float32
 BF16 = mybir.dt.bfloat16
@@ -45,10 +47,6 @@ def tile_matchingnet_pa_kernel(tc, h3, W4, b4, W5_bytes, W5_scale, b5, out):
         nc.vector.tensor_reduce(out=par[:], in_=idq, axis=mybir.AxisListType.XY, op=ALU.add)
         pv = keep.tile([P, P], F32, name="pv")
         pu = keep.tile([P, P], F32, name="pu")
-        pf = keep.tile([P, P], F32, name="pf")
-        nc.gpsimd.tensor_copy(
-            out=pf[:].rearrange("p (b c k) -> p b c k", b=4, c=NCH), in_=ident[:].rearrange("p (k c b) -> p b c k", k=4, c=NCH)
-        )
         pvv = pv[:].rearrange("p (h e c a k) -> p h e c a k", h=2, e=2, c=NCH, a=2)
         puv = pu[:].rearrange("p (h e c a k) -> p h e c a k", h=2, e=2, c=NCH, a=2)
         iv = ident[:].rearrange("p (h e c g a) -> p h e c g a", h=2, e=2, c=NCH, g=2)
@@ -61,6 +59,8 @@ def tile_matchingnet_pa_kernel(tc, h3, W4, b4, W5_bytes, W5_scale, b5, out):
                     nc.gpsimd.tensor_copy(out=puv[:, x, e, :, :, k], in_=iu[:, x, k, :, :, g])
         ones = keep.tile([P, 1], F32, name="ones")
         nc.gpsimd.memset(ones[:], 1.0)
+        scratch = keep.tile([P, 1], F32, name="scratch")
+        nc.scalar.activation(out=scratch[:], in_=ones[:], func=ACT.Exp)
         b4h = keep.tile([P, G, PACK], BF16, name="b4h")
         b4c = keep.tile([P, G * PACK], F32, name="b4c")
         sc5 = keep.tile([P, G, PACK], F32, name="sc5")
@@ -241,8 +241,8 @@ def tile_matchingnet_pa_kernel(tc, h3, W4, b4, W5_bytes, W5_scale, b5, out):
         def logs(e):
             nc.scalar.activation(out=e[:], in_=e[:], func=ACT.Ln, bias=ones[:, 0:1])
 
-        def mov(t, rows, R):
-            return t[rows, :].rearrange("p (s t h x) -> p s t h x", t=2, h=R, x=R)
+        def mov(t, rows):
+            return t[rows, :].rearrange("p (s t h x) -> p s t h x", t=2, h=2, x=2)
 
         def transposes(dst, src, n):
             for h in range(n // 8):
@@ -253,7 +253,6 @@ def tile_matchingnet_pa_kernel(tc, h3, W4, b4, W5_bytes, W5_scale, b5, out):
                 nc.scalar.copy(out=dst[:, DOUT * h : DOUT * (h + 1)], in_=bb)
 
         def blocks(z, l, m):
-            R = 4 if m == 0 else 2
             K = late.tile([P, DOUT], F32, name="K", bufs=4, align_bytes=64)
             nc.vector.scalar_tensor_tensor(out=K[:], in0=l[:], scalar=40.0, in1=z[:], op0=ALU.min, op1=ALU.max)
             Yp = late.tile([P, DOUT], F32, name="Yp", bufs=2, align_bytes=64)
@@ -269,42 +268,37 @@ def tile_matchingnet_pa_kernel(tc, h3, W4, b4, W5_bytes, W5_scale, b5, out):
             hl = late.tile([P, 2, DOUT], BF16, name="hl", bufs=3)
             nc.scalar.copy(out=hl[:, 0], in_=Yc[:])
             nc.vector.tensor_tensor(out=hl[:, 1], in0=Yc[:], in1=hl[:, 0], op=ALU.subtract)
-            if R == 4:
-                ys = hl[:].rearrange("p w (c n) -> p (w c) n", n=P)
-                xt = late.tile([P, 2 * NCH * P], BF16, name="xt")
-            else:
-                yt = late.tile([P, 2 * NCH, 2, P], BF16, name="yt", bufs=3)
-                src = hl[:].rearrange("p w (c a k i) -> p (w c) a k i", a=2, k=2, i=N)
-                for sg in range(2):
-                    for kp in range(2):
-                        r = (sg + kp) % 2
-                        nc.vector.tensor_scalar(
-                            out=yt[:, :, sg, :].rearrange("p w (a k i) -> p w a k i", a=2, k=2)[:, :, :, kp, :],
-                            in0=src[:, :, :, kp, :],
-                            scalar1=par[:, r : r + 1],
-                            scalar2=None,
-                            op0=ALU.mult,
-                        )
-                ys = yt[:].rearrange("p w g n -> p (w g) n")
-                xt = late.tile([P, 4 * NCH * P], BF16, name="xh", bufs=3)
-            return dict(K=K, ys=ys, xt=xt, m=m, R=R)
+            yt = late.tile([P, 2 * NCH, 2, P], BF16, name="yt", bufs=4)
+            src = hl[:].rearrange("p w (c a k i) -> p (w c) a k i", a=2, k=2, i=N)
+            for sg in range(2):
+                for kp in range(2):
+                    r = (sg + kp) % 2
+                    nc.vector.tensor_scalar(
+                        out=yt[:, :, sg, :].rearrange("p w (a k i) -> p w a k i", a=2, k=2)[:, :, :, kp, :],
+                        in0=src[:, :, :, kp, :],
+                        scalar1=par[:, r : r + 1],
+                        scalar2=None,
+                        op0=ALU.mult,
+                    )
+            ys = yt[:].rearrange("p w g n -> p (w g) n")
+            xt = late.tile([P, 4 * NCH * P], BF16, name="xh", bufs=4)
+            return dict(K=K, ys=ys, xt=xt, m=m)
 
-        def state(s):
-            R, m, xt = s["R"], s["m"], s["xt"]
-            transposes(xt, s["ys"], 64 // R)
-            ub = late.tile([P, 2 * N * R], BF16, name="ub%d" % m)
-            vb = late.tile([P, 2 * N * R], BF16, name="vb%d" % m)
+        def pair_state(tiles, k):
+            for s in tiles:
+                transposes(s["xt"], s["ys"], 32)
+                s["xs"] = s["xt"][:].rearrange("p (w n) -> p w n", n=P)
+            ub = late.tile([P, 2 * SEQ], BF16, name="ub%d" % k)
+            vb = late.tile([P, 2 * SEQ], BF16, name="vb%d" % k)
             nc.gpsimd.memset(ub[:], 0.0)
             nc.gpsimd.memset(vb[:], 0.0)
-            for g in range(R):
-                rows = slice(P // R * g, P // R * (g + 1))
-                nc.gpsimd.memset(mov(ub, rows, R)[:, :, 0, g, :], 1.0)
-            wu = late.tile([P, N], F32, name="wu%d" % m, align_bytes=64)
-            wv = late.tile([P, N], F32, name="wv%d" % m, align_bytes=64)
+            for g, rows in enumerate(HALVES):
+                nc.gpsimd.memset(mov(ub, rows)[:, :, 0, g, :], 1.0)
+            wu = late.tile([P, 2 * N], F32, name="wu%d" % k, align_bytes=64)
+            wv = late.tile([P, 2 * N], F32, name="wv%d" % k, align_bytes=64)
             nc.gpsimd.memset(wu[:], 1.0)
             nc.gpsimd.memset(wv[:], 1.0)
-            s["xs"] = xt[:].rearrange("p (w n) -> p w n", n=P)
-            s["ub"], s["vb"], s["wu"], s["wv"] = ub, vb, wu, wv
+            return dict(tiles=tiles, ub=ub, vb=vb, wu=wu, wv=wv)
 
         def keep_warm(n):
             for k in range(n):
@@ -318,40 +312,44 @@ def tile_matchingnet_pa_kernel(tc, h3, W4, b4, W5_bytes, W5_scale, b5, out):
                     stop=True,
                 )
 
-        def half_step(mat, src, dst, w, R):
-            n = R * R
-            ns = N // R
+        def half_step(s, key, src, dst, w):
             bank = psum.tile([P, HALF], F32, name="bank", bufs=NBANK)
-            for s in range(ns):
-                o = 2 * n * s
-                nc.tensor.matmul(
-                    out=bank[:, o : o + 2 * n], lhsT=mat[:, s, :], rhs=src[:, o : o + 2 * n], start=True, stop=False
+            for k, tile in enumerate(s["tiles"]):
+                mat = tile[key]
+                for c in range(2 * NCH):
+                    o = SEQ * k + 8 * c
+                    nc.tensor.matmul(
+                        out=bank[:, o : o + 8], lhsT=mat[:, c, :], rhs=src[:, o : o + 8], start=True, stop=False
+                    )
+                    nc.tensor.matmul(
+                        out=bank[:, o : o + 4],
+                        lhsT=mat[:, 2 * NCH + c, :],
+                        rhs=src[:, o : o + 4],
+                        start=False,
+                        stop=True,
+                    )
+            keep_warm(3)
+            part = late.tile([P, 2, 2 * N], F32, name="part", bufs=4)
+            for g, rows in enumerate(HALVES):
+                nc.scalar.copy(
+                    out=part[rows].rearrange("p t (s a) -> p t s a", a=2),
+                    in_=bank[rows, 0 : 2 * SEQ].rearrange("p (s t a x) -> p t s a x", t=2, a=2, x=2)[:, :, :, :, g],
                 )
-                nc.tensor.matmul(
-                    out=bank[:, o : o + n], lhsT=mat[:, ns + s, :], rhs=src[:, o : o + n], start=False, stop=True
-                )
-            t = late.tile([P, N], F32, name="t", bufs=8)
-            groups = [slice(P // R * g, P // R * (g + 1)) for g in range(R)]
-            for g, rows in enumerate(groups):
-                nc.vector.tensor_reduce(
-                    out=t[rows, :].rearrange("p (s a) -> p s a", a=R),
-                    in_=bank[rows, 0 : 2 * n * ns].rearrange("p (s t a x) -> p s a x t", t=2, a=R, x=R)[:, :, :, g, :],
-                    axis=mybir.AxisListType.X,
-                    op=ALU.add,
-                )
+            t = late.tile([P, 2 * N], F32, name="t", bufs=4)
+            nc.vector.tensor_tensor(out=t[:], in0=part[:, 0], in1=part[:, 1], op=ALU.add)
             nc.vector.scalar_tensor_tensor(out=w[:], in0=w[:], scalar=EPS, in1=t[:], op0=ALU.mult, op1=ALU.max)
-            v = late.tile([P, N], F32, name="v", bufs=8, align_bytes=64)
+            v = late.tile([P, 2 * N], F32, name="v", bufs=4, align_bytes=64)
             nc.vector.reciprocal(out=v[:], in_=w[:])
             if dst is not None:
-                for g, rows in enumerate(groups):
+                for g, rows in enumerate(HALVES):
                     nc.scalar.copy(
-                        out=mov(dst, rows, R)[:, :, 0, g, :], in_=v[rows, :].rearrange("p (s a) -> p s a", a=R)
+                        out=mov(dst, rows)[:, :, 0, g, :], in_=v[rows, :].rearrange("p (s a) -> p s a", a=2)
                     )
-                for g, rows in enumerate(groups):
-                    nc.vector.tensor_tensor(
-                        out=mov(dst, rows, R)[:, :, 1, g, :],
-                        in0=v[rows, :].rearrange("p (s a) -> p s a", a=R),
-                        in1=mov(dst, rows, R)[:, :, 0, g, :],
+                for g, rows in enumerate(HALVES):
+                    nc.gpsimd.tensor_tensor(
+                        out=mov(dst, rows)[:, :, 1, g, :],
+                        in0=v[rows, :].rearrange("p (s a) -> p s a", a=2),
+                        in1=mov(dst, rows)[:, :, 0, g, :],
                         op=ALU.subtract,
                     )
             return v
@@ -363,9 +361,9 @@ def tile_matchingnet_pa_kernel(tc, h3, W4, b4, W5_bytes, W5_scale, b5, out):
             nc.tensor.matmul(out=bank[:, 0:N], lhsT=perm[:], rhs=vt[:], start=True, stop=True)
             return bank
 
-        def finish(s, v):
-            vn = natural(v[:], ident if s["R"] == 4 else pv)
-            wn = natural(s["wu"][:], pf if s["R"] == 4 else pu)
+        def finish(s, v, wu):
+            vn = natural(v, pv)
+            wn = natural(wu, pu)
             kv = late.tile([P, N, N], F32, name="kv", bufs=2)
             nc.vector.tensor_tensor(
                 out=kv[:],
@@ -390,35 +388,35 @@ def tile_matchingnet_pa_kernel(tc, h3, W4, b4, W5_bytes, W5_scale, b5, out):
                 nc.sync.dma_start(out=out[P * m : P * (m + 1), ii, :], in_=res[:, ii])
 
         warm = psum.tile([P, HALF], F32, name="warm")
-        SKEW = 0
+        LAG = 0
         STEPS = 2 * ITERS - 1
         zs = [logits(m) for m in range(TT)]
         es = [None] * TT
-        for pair in range(2):
-            for m in (2 * pair, 2 * pair + 1):
-                es[m] = exps(zs[m])
-            for m in (2 * pair, 2 * pair + 1):
-                logs(es[m])
-        st = [None] * TT
+        for m in range(TT):
+            es[m] = exps(zs[m])
+        for m in range(TT):
+            logs(es[m])
+        st = [None] * 2
 
         def one_step(s, h):
             end = h == STEPS - 1
             if h % 2 == 0:
-                v = half_step(s["xs"], s["ub"], None if end else s["vb"], s["wv"], s["R"])
+                v = half_step(s, "xs", s["ub"], None if end else s["vb"], s["wv"])
                 if end:
-                    finish(s, v)
+                    for k, tile in enumerate(s["tiles"]):
+                        cols = slice(N * k, N * (k + 1))
+                        finish(tile, v[:, cols], s["wu"][:, cols])
             else:
-                half_step(s["ys"], s["vb"], s["ub"], s["wu"], s["R"])
+                half_step(s, "ys", s["vb"], s["ub"], s["wu"])
 
         with tc.manual_schedule(engines={mybir.EngineType.PE}):
-            for r in range(STEPS + SKEW * (TT - 1)):
-                for m in range(TT):
-                    h = r - SKEW * m
+            for r in range(STEPS + LAG):
+                for k in range(2):
+                    h = r - LAG * k
                     if h == 0:
-                        st[m] = blocks(zs[m], es[m], m)
-                        state(st[m])
+                        st[k] = pair_state([blocks(zs[m], es[m], m) for m in (2 * k, 2 * k + 1)], k)
                         keep_warm(6)
                     if 0 <= h < STEPS:
-                        one_step(st[m], h)
-                        if m in (1, 3):
-                            keep_warm(1)
+                        one_step(st[k], h)
+                if r >= LAG and r % 4 == 0:
+                    keep_warm(4)

from contextlib import ExitStack

import concourse.mybir as mybir
from concourse.masks import make_identity

B, HID, N = 512, 2048, 32
DOUT = N * N
ITERS = 10
SLOPE = 0.01
EPS = 1e-8

FLOPS = 2 * B * HID * (HID + DOUT)

P = 128
PACK = 4
KP = P * PACK
G = HID // KP
TT = B // P
HALF = 512
NCH = 8
SEQ = 16 * NCH
NBANK = 7
HALVES = (slice(0, 64), slice(64, 128))

F32 = mybir.dt.float32
BF16 = mybir.dt.bfloat16
U32 = mybir.dt.uint32
U8 = mybir.dt.uint8
X4 = mybir.dt.float8_e4m3fn_x4
FP8 = mybir.dt.float8_e4m3fn
ACT = mybir.ActivationFunctionType
ALU = mybir.AluOpType


def tile_matchingnet_pa_kernel(tc, h3, W4, b4, W5_bytes, W5_scale, b5, out):
    nc = tc.nc
    with ExitStack() as ctx:
        keep = ctx.enter_context(tc.tile_pool(name="keep", bufs=1))
        psum = ctx.enter_context(tc.psum_pool(name="psum", bufs=1))

        ident = keep.tile([P, P], F32, name="ident")
        make_identity(nc, ident[:])
        identb = keep.tile([P, P], BF16, name="identb")
        make_identity(nc, identb[:])
        par = keep.tile([P, 2], F32, name="par")
        idq = ident[:].rearrange("p (a b r) -> p b a r", a=2, b=2)
        nc.vector.tensor_reduce(out=par[:], in_=idq, axis=mybir.AxisListType.XY, op=ALU.add)
        pv = keep.tile([P, P], F32, name="pv")
        pu = keep.tile([P, P], F32, name="pu")
        pvv = pv[:].rearrange("p (h e c a k) -> p h e c a k", h=2, e=2, c=NCH, a=2)
        puv = pu[:].rearrange("p (h e c a k) -> p h e c a k", h=2, e=2, c=NCH, a=2)
        iv = ident[:].rearrange("p (h e c g a) -> p h e c g a", h=2, e=2, c=NCH, g=2)
        iu = ident[:].rearrange("p (a k c g x) -> p x k c a g", a=2, k=2, c=NCH, g=2)
        for e in range(2):
            for k in range(2):
                g = (e + k) % 2
                for x in range(2):
                    nc.gpsimd.tensor_copy(out=pvv[:, x, e, :, :, k], in_=iv[:, x, e, :, g, :])
                    nc.gpsimd.tensor_copy(out=puv[:, x, e, :, :, k], in_=iu[:, x, k, :, :, g])
        ones = keep.tile([P, 1], F32, name="ones")
        nc.gpsimd.memset(ones[:], 1.0)
        scratch = keep.tile([P, 1], F32, name="scratch")
        nc.scalar.activation(out=scratch[:], in_=ones[:], func=ACT.Exp)
        b4h = keep.tile([P, G, PACK], BF16, name="b4h")
        b4c = keep.tile([P, G * PACK], F32, name="b4c")
        sc5 = keep.tile([P, G, PACK], F32, name="sc5")
        b5r = keep.tile([P, DOUT], BF16, name="b5r")

        h3c = [keep.tile([P, B], U32, name="h3c%d" % g, align_bytes=64) for g in range(G)]
        h3s = [keep.tile([P, B], U8, name="h3s%d" % g, align_bytes=64) for g in range(G)]
        w5c = [keep.tile([P, DOUT], U32, name="w5c%d" % g, align_bytes=64) for g in range(G)]
        w5s = [keep.tile([P, DOUT], U8, name="w5s%d" % g, align_bytes=64) for g in range(G)]
        h4c = [keep.tile([P, B], U32, name="h4c%d" % g, align_bytes=64) for g in range(G)]
        h4s = [keep.tile([P, B], U8, name="h4s%d" % g, align_bytes=64) for g in range(G)]

        with ExitStack() as fctx:
            front = fctx.enter_context(tc.tile_pool(name="front", bufs=1))
            hraw = [front.tile([P, HID], BF16, name="hraw%d" % m) for m in range(TT)]
            gx = front.tile([P, G, B, PACK], BF16, name="gx", align_bytes=64)

            def load_w4(c, g):
                raw = front.tile([P, PACK, HALF], BF16, name="w4raw", bufs=8)
                nc.sync.dma_start(
                    out=raw[:],
                    in_=W4[KP * g : KP * (g + 1), HALF * c : HALF * (c + 1)].rearrange("(p j) n -> p j n", j=PACK),
                )
                return raw

            def load_w5(g):
                byt = front.tile([P, PACK, DOUT], U8, name="w5b", bufs=2)
                nc.sync.dma_start(out=byt[:], in_=W5_bytes[KP * g : KP * (g + 1), :].rearrange("(p j) n -> p j n", j=PACK))
                return byt

            nc.scalar.dma_start(out=b4h[:], in_=b4.rearrange("(g p j) -> p g j", p=P, j=PACK))
            nc.scalar.dma_start(out=sc5[:], in_=W5_scale.rearrange("(g p j) o -> p g (j o)", p=P, j=PACK))
            nc.gpsimd.tensor_copy(out=b4c[:], in_=b4h[:].rearrange("p g j -> p (g j)"))

            w4raw = {}
            w5byt = {}
            w5byt[0] = load_w5(0)
            w4raw[0, 0] = load_w4(0, 0)
            for m in range(TT):
                nc.sync.dma_start(out=hraw[m][:], in_=h3[P * m : P * (m + 1), :])
            for g in range(1, G):
                w4raw[0, g] = load_w4(0, g)

            def h3_tile(m):
                words = hraw[m][:].bitcast(F32)
                gxw = gx[:].bitcast(F32)
                for gp in range(G // 2):
                    bank = psum.tile([P, HALF], F32, name="bank", bufs=NBANK)
                    for gg in range(2):
                        for u in range(2):
                            g = 2 * gp + gg
                            s = 2 * gg + u
                            nc.tensor.transpose(
                                bank[:, P * s : P * (s + 1)], words[:, 256 * g + u : 256 * (g + 1) : 2], ident[:]
                            )
                    for gg in range(2):
                        nc.scalar.copy(
                            out=gxw[:, 2 * gp + gg, P * m : P * (m + 1), :],
                            in_=bank[:, 256 * gg : 256 * (gg + 1)].rearrange("p (u r) -> p r u", u=2),
                        )

            def prep_w4(c, g, codes, scales):
                raw = w4raw.pop((c, g))
                grp = front.tile([P, PACK, P, PACK], BF16, name="w4grp", bufs=4, align_bytes=64)
                src = raw[:].rearrange("p j (m t) -> p t m j", t=PACK)
                nc.vector.tensor_copy(out=grp[:, 0:2], in_=src[:, 0:2])
                nc.scalar.copy(out=grp[:, 2:4], in_=src[:, 2:4])
                nc.vector.quantize_mx(
                    out=codes[:].bitcast(X4), scales=scales[:], in_=grp[:].rearrange("p t m j -> p (t m j)")
                )

            def prep_w5(g):
                byt = w5byt.pop(g)
                wide = front.tile([P, PACK, DOUT], BF16, name="w5p", bufs=2)
                for j in range(PACK):
                    nc.scalar.activation(
                        out=wide[:, j, :], in_=byt[:, j, :].bitcast(FP8), func=ACT.Copy, scale=sc5[:, g, j : j + 1]
                    )
                for h in range(2):
                    grp = front.tile([P, HALF, PACK], BF16, name="w5g", bufs=3, align_bytes=64)
                    nc.vector.tensor_copy(
                        out=grp[:], in_=wide[:, :, HALF * h : HALF * (h + 1)].rearrange("p j n -> p n j")
                    )
                    cols = slice(HALF * h, HALF * (h + 1))
                    nc.vector.quantize_mx(
                        out=w5c[g][:, cols].bitcast(X4), scales=w5s[g][:, cols], in_=grp[:].rearrange("p n j -> p (n j)")
                    )

            prep_w5(0)
            for m in range(TT):
                h3_tile(m)
            for g in range(G):
                nc.vector.quantize_mx(
                    out=h3c[g][:].bitcast(X4), scales=h3s[g][:], in_=gx[:, g].rearrange("p n t -> p (n t)")
                )

            def front_chunk(c):
                codes = []
                scales = []
                for g in range(G):
                    cw = front.tile([P, HALF], U32, name="w4c%d" % g, bufs=2, align_bytes=64)
                    sw = front.tile([P, HALF], U8, name="w4s%d" % g, bufs=2, align_bytes=64)
                    prep_w4(c, g, cw, sw)
                    codes.append(cw)
                    scales.append(sw)
                y = front.tile([P, PACK, B], F32, name="y", bufs=2)
                banks = [psum.tile([P, HALF], F32, name="bank", bufs=NBANK) for t in range(PACK)]
                for g in range(G):
                    for t in range(PACK):
                        mc = slice(P * t, P * (t + 1))
                        nc.tensor.matmul_mx(
                            out=banks[t][:],
                            lhsT=codes[g][:, mc].bitcast(X4),
                            lhsT_scale=scales[g][:, mc],
                            rhs=h3c[g][:].bitcast(X4),
                            rhs_scale=h3s[g][:],
                            start=(g == 0),
                            stop=(g == G - 1),
                        )
                for t in range(PACK):
                    nc.scalar.activation(
                        out=y[:, t, :],
                        in_=banks[t][:],
                        func=ACT.Identity,
                        bias=b4c[:, PACK * c + t : PACK * c + t + 1],
                    )
                hb = front.tile([P, B, PACK], BF16, name="hb", bufs=2, align_bytes=64)
                yv = y[:].rearrange("p t n -> p n t")
                for h in range(2):
                    tok = slice(256 * h, 256 * (h + 1))
                    nc.vector.scalar_tensor_tensor(
                        out=hb[:, tok], in0=yv[:, tok], scalar=SLOPE, in1=yv[:, tok], op0=ALU.mult, op1=ALU.max
                    )
                    nc.vector.quantize_mx(
                        out=h4c[c][:, tok].bitcast(X4),
                        scales=h4s[c][:, tok],
                        in_=hb[:, tok].rearrange("p n t -> p (n t)"),
                    )

            for c in range(G):
                if c + 1 < G:
                    for g in range(G):
                        w4raw[c + 1, g] = load_w4(c + 1, g)
                    w5byt[c + 1] = load_w5(c + 1)
                if c == G - 1:
                    nc.sync.dma_start(out=b5r[:], in_=b5.partition_broadcast(P))
                front_chunk(c)
                if c > 0:
                    prep_w5(c)

        late = ctx.enter_context(tc.tile_pool(name="late", bufs=1))

        def logits(m):
            z = late.tile([P, DOUT], F32, name="z", bufs=4)
            banks = [psum.tile([P, HALF], F32, name="bank", bufs=NBANK) for h in range(2)]
            for g in range(G):
                for h in range(2):
                    cols = slice(HALF * h, HALF * (h + 1))
                    nc.tensor.matmul_mx(
                        out=banks[h][:],
                        lhsT=h4c[g][:, P * m : P * (m + 1)].bitcast(X4),
                        lhsT_scale=h4s[g][:, P * m : P * (m + 1)],
                        rhs=w5c[g][:, cols].bitcast(X4),
                        rhs_scale=w5s[g][:, cols],
                        start=(g == 0),
                        stop=(g == G - 1),
                    )
            for h in range(2):
                cols = slice(HALF * h, HALF * (h + 1))
                nc.vector.tensor_tensor(out=z[:, cols], in0=banks[h][:], in1=b5r[:, cols], op=ALU.add)
            return z

        def exps(z):
            e = late.tile([P, DOUT], F32, name="e", bufs=4)
            nc.scalar.activation(out=e[:], in_=z[:], func=ACT.Exp)
            return e

        def logs(e):
            nc.scalar.activation(out=e[:], in_=e[:], func=ACT.Ln, bias=ones[:, 0:1])

        def mov(t, rows):
            return t[rows, :].rearrange("p (s t h x) -> p s t h x", t=2, h=2, x=2)

        def transposes(dst, src, n):
            for h in range(n // 8):
                bank = psum.tile([P, HALF], F32, name="bank", bufs=NBANK)
                bb = bank[:].bitcast(BF16)
                for c in range(8):
                    nc.tensor.transpose(bb[:, P * c : P * (c + 1)], src[:, 8 * h + c, :], identb[:])
                nc.scalar.copy(out=dst[:, DOUT * h : DOUT * (h + 1)], in_=bb)

        def blocks(z, l, m):
            K = late.tile([P, DOUT], F32, name="K", bufs=4, align_bytes=64)
            nc.vector.scalar_tensor_tensor(out=K[:], in0=l[:], scalar=40.0, in1=z[:], op0=ALU.min, op1=ALU.max)
            Yp = late.tile([P, DOUT], F32, name="Yp", bufs=2, align_bytes=64)
            nc.vector.transpose(out=Yp[:], in_=K[:])
            Yc = late.tile([P, DOUT], F32, name="Yc", bufs=2)
            nc.vector.tensor_scalar(
                out=Yc[:].rearrange("p (b i) -> p b i", i=N),
                in0=Yp[:].rearrange("p (i b) -> p b i", b=N),
                scalar1=1e-20,
                scalar2=None,
                op0=ALU.max,
            )
            hl = late.tile([P, 2, DOUT], BF16, name="hl", bufs=3)
            nc.scalar.copy(out=hl[:, 0], in_=Yc[:])
            nc.vector.tensor_tensor(out=hl[:, 1], in0=Yc[:], in1=hl[:, 0], op=ALU.subtract)
            yt = late.tile([P, 2 * NCH, 2, P], BF16, name="yt", bufs=4)
            src = hl[:].rearrange("p w (c a k i) -> p (w c) a k i", a=2, k=2, i=N)
            for sg in range(2):
                for kp in range(2):
                    r = (sg + kp) % 2
                    nc.vector.tensor_scalar(
                        out=yt[:, :, sg, :].rearrange("p w (a k i) -> p w a k i", a=2, k=2)[:, :, :, kp, :],
                        in0=src[:, :, :, kp, :],
                        scalar1=par[:, r : r + 1],
                        scalar2=None,
                        op0=ALU.mult,
                    )
            ys = yt[:].rearrange("p w g n -> p (w g) n")
            xt = late.tile([P, 4 * NCH * P], BF16, name="xh", bufs=4)
            return dict(K=K, ys=ys, xt=xt, m=m)

        def pair_state(tiles, k):
            for s in tiles:
                transposes(s["xt"], s["ys"], 32)
                s["xs"] = s["xt"][:].rearrange("p (w n) -> p w n", n=P)
            ub = late.tile([P, 2 * SEQ], BF16, name="ub%d" % k)
            vb = late.tile([P, 2 * SEQ], BF16, name="vb%d" % k)
            nc.gpsimd.memset(ub[:], 0.0)
            nc.gpsimd.memset(vb[:], 0.0)
            for g, rows in enumerate(HALVES):
                nc.gpsimd.memset(mov(ub, rows)[:, :, 0, g, :], 1.0)
            wu = late.tile([P, 2 * N], F32, name="wu%d" % k, align_bytes=64)
            wv = late.tile([P, 2 * N], F32, name="wv%d" % k, align_bytes=64)
            nc.gpsimd.memset(wu[:], 1.0)
            nc.gpsimd.memset(wv[:], 1.0)
            return dict(tiles=tiles, ub=ub, vb=vb, wu=wu, wv=wv)

        def keep_warm(n):
            for k in range(n):
                nc.tensor.matmul_mx(
                    out=warm[:],
                    lhsT=h4c[0][:, 0:P].bitcast(X4),
                    lhsT_scale=h4s[0][:, 0:P],
                    rhs=w5c[0][:, 0:HALF].bitcast(X4),
                    rhs_scale=w5s[0][:, 0:HALF],
                    start=True,
                    stop=True,
                )

        def half_step(s, key, src, dst, w):
            bank = psum.tile([P, HALF], F32, name="bank", bufs=NBANK)
            for k, tile in enumerate(s["tiles"]):
                mat = tile[key]
                for c in range(2 * NCH):
                    o = SEQ * k + 8 * c
                    nc.tensor.matmul(
                        out=bank[:, o : o + 8], lhsT=mat[:, c, :], rhs=src[:, o : o + 8], start=True, stop=False
                    )
                    nc.tensor.matmul(
                        out=bank[:, o : o + 4],
                        lhsT=mat[:, 2 * NCH + c, :],
                        rhs=src[:, o : o + 4],
                        start=False,
                        stop=True,
                    )
            keep_warm(3)
            part = late.tile([P, 2, 2 * N], F32, name="part", bufs=4)
            for g, rows in enumerate(HALVES):
                nc.scalar.copy(
                    out=part[rows].rearrange("p t (s a) -> p t s a", a=2),
                    in_=bank[rows, 0 : 2 * SEQ].rearrange("p (s t a x) -> p t s a x", t=2, a=2, x=2)[:, :, :, :, g],
                )
            t = late.tile([P, 2 * N], F32, name="t", bufs=4)
            nc.vector.tensor_tensor(out=t[:], in0=part[:, 0], in1=part[:, 1], op=ALU.add)
            nc.vector.scalar_tensor_tensor(out=w[:], in0=w[:], scalar=EPS, in1=t[:], op0=ALU.mult, op1=ALU.max)
            v = late.tile([P, 2 * N], F32, name="v", bufs=4, align_bytes=64)
            nc.vector.reciprocal(out=v[:], in_=w[:])
            if dst is not None:
                for g, rows in enumerate(HALVES):
                    nc.scalar.copy(
                        out=mov(dst, rows)[:, :, 0, g, :], in_=v[rows, :].rearrange("p (s a) -> p s a", a=2)
                    )
                for g, rows in enumerate(HALVES):
                    nc.gpsimd.tensor_tensor(
                        out=mov(dst, rows)[:, :, 1, g, :],
                        in0=v[rows, :].rearrange("p (s a) -> p s a", a=2),
                        in1=mov(dst, rows)[:, :, 0, g, :],
                        op=ALU.subtract,
                    )
            return v

        def natural(v, perm):
            vt = late.tile([P, N], F32, name="vt", bufs=4, align_bytes=64)
            nc.vector.transpose(out=vt[:], in_=v)
            bank = psum.tile([P, HALF], F32, name="bank", bufs=NBANK)
            nc.tensor.matmul(out=bank[:, 0:N], lhsT=perm[:], rhs=vt[:], start=True, stop=True)
            return bank

        def finish(s, v, wu):
            vn = natural(v, pv)
            wn = natural(wu, pu)
            kv = late.tile([P, N, N], F32, name="kv", bufs=2)
            nc.vector.tensor_tensor(
                out=kv[:],
                in0=s["K"][:].rearrange("p (i j) -> p i j", j=N),
                in1=vn[:, 0:N].unsqueeze(1).to_broadcast([P, N, N]),
                op=ALU.mult,
            )
            rs = late.tile([P, N], F32, name="rs", bufs=2)
            nc.vector.tensor_reduce(out=rs[:], in_=kv[:], axis=mybir.AxisListType.X, op=ALU.add)
            nc.vector.scalar_tensor_tensor(
                out=rs[:], in0=wn[:, 0:N], scalar=EPS, in1=rs[:], op0=ALU.mult, op1=ALU.max
            )
            un = late.tile([P, N], F32, name="un", bufs=2)
            nc.vector.reciprocal(out=un[:], in_=rs[:])
            res = late.tile([P, N, N], F32, name="res", bufs=2)
            m = s["m"]
            for h in range(2):
                ii = slice(16 * h, 16 * h + 16)
                nc.vector.tensor_tensor(
                    out=res[:, ii], in0=kv[:, ii], in1=un[:, ii].unsqueeze(2).to_broadcast([P, 16, N]), op=ALU.mult
                )
                nc.sync.dma_start(out=out[P * m : P * (m + 1), ii, :], in_=res[:, ii])

        warm = psum.tile([P, HALF], F32, name="warm")
        LAG = 0
        STEPS = 2 * ITERS - 1
        zs = [logits(m) for m in range(TT)]
        es = [None] * TT
        for m in range(TT):
            es[m] = exps(zs[m])
        for m in range(TT):
            logs(es[m])
        st = [None] * 2

        def one_step(s, h):
            end = h == STEPS - 1
            if h % 2 == 0:
                v = half_step(s, "xs", s["ub"], None if end else s["vb"], s["wv"])
                if end:
                    for k, tile in enumerate(s["tiles"]):
                        cols = slice(N * k, N * (k + 1))
                        finish(tile, v[:, cols], s["wu"][:, cols])
            else:
                half_step(s, "ys", s["vb"], s["ub"], s["wu"])

        with tc.manual_schedule(engines={mybir.EngineType.PE}):
            for r in range(STEPS + LAG):
                for k in range(2):
                    h = r - LAG * k
                    if h == 0:
                        st[k] = pair_state([blocks(zs[m], es[m], m) for m in (2 * k, 2 * k + 1)], k)
                        keep_warm(6)
                    if 0 <= h < STEPS:
                        one_step(st[k], h)
                if r >= LAG and r % 4 == 0:
                    keep_warm(4)
